import numpy as np
import ml_dtypes


def mxq(x, axis, fmt="e4m3"):
    dtype, down = {"e4m3": (ml_dtypes.float8_e4m3fn, 7), "e5m2": (ml_dtypes.float8_e5m2, 14)}[fmt]
    v = np.moveaxis(np.asarray(x, np.float32).astype(ml_dtypes.bfloat16).astype(np.float64), axis, -1)
    blocks = v.reshape(v.shape[:-1] + (-1, 32))
    amax = np.abs(blocks).max(-1, keepdims=True)
    byte = np.maximum(np.where(amax > 0, np.frexp(amax)[1] - 1 + 127, 0) - down, 1)
    scale = np.exp2(byte - 127.0)
    codes = (blocks / scale).astype(np.float32).astype(dtype).astype(np.float64)
    return np.moveaxis((codes * scale).reshape(v.shape), -1, axis)


WIDE = False


def mx_kscale(k):
    if not WIDE:
        return np.ones(k)
    levels = np.array([10, -10, 5, -5, 0])
    a = np.random.permutation(np.resize(levels, k // 512 * 4)).reshape(k // 512, 4)
    idx = np.arange(k)
    return np.exp2(a[idx // 512, idx % 128 // 32])


BF16 = ml_dtypes.bfloat16


def bf(x):
    return np.asarray(x, np.float32).astype(BF16)


def f64(x):
    return np.asarray(x).astype(np.float64)


N, L, C, M = 2, 512, 1024, 512
T = N * L
EPS_ATTN = 1e-8


def softmax_rows(v):
    e = np.exp(v - v.max(axis=-1, keepdims=True))
    return e / e.sum(axis=-1, keepdims=True)


def setup_inputs():
    s = mx_kscale(C)
    mem = np.random.standard_normal((M, C))
    mem = mem / np.linalg.norm(mem, axis=1, keepdims=True)
    return {"q": bf(np.random.standard_normal((T, C)) * s), "mem": bf(mem / s)}


def reference(q, mem):
    qf, m = f64(q), f64(mem)
    sc = mxq(qf, 1, "e4m3") @ mxq(m, 1, "e4m3").T
    attn_u = np.maximum(softmax_rows(sc), EPS_ATTN)
    return mxq(attn_u, 0, "e4m3").T @ mxq(qf, 0, "e4m3")

@@ -1,0 +1,212 @@
+from contextlib import ExitStack
+
+import concourse.masks as masks
+import concourse.mybir as mybir
+
+F32 = mybir.dt.float32
+BF16 = mybir.dt.bfloat16
+U32 = mybir.dt.uint32
+U8 = mybir.dt.uint8
+FP8X4 = mybir.dt.float8_e4m3fn_x4
+ACT = mybir.ActivationFunctionType
+ALU = mybir.AluOpType
+AXIS = mybir.AxisListType
+
+P = 128
+PACK = 4
+K_PASS = P * PACK
+N_BANK = 512
+
+TOKENS = 1024
+WIDTH = 1024
+SLOTS = 512
+FLOOR = 1e-8
+
+TOKEN_PASSES = TOKENS // K_PASS
+WIDTH_PASSES = WIDTH // K_PASS
+TOKEN_TILES = TOKENS // P
+SLOT_TILES = SLOTS // P
+WIDTH_HALVES = WIDTH // N_BANK
+PAIR = 2
+WORDS = WIDTH // PAIR
+RUN = 4
+
+FLOPS = 2 * 2 * TOKENS * WIDTH * SLOTS
+
+
+def flip_rows(nc, banks, identity, row_words, grouped_words, copy):
+    flipped = banks.tile([P, WIDTH_PASSES, PAIR, P], F32, tag="bank")
+    for h in range(WIDTH_PASSES):
+        for u in range(PAIR):
+            first = (h * PAIR + u) * P
+            nc.tensor.transpose(flipped[:, h, u, :], row_words[:, first : first + P], identity[:])
+    copy(out=grouped_words, in_=flipped[:].rearrange("p h u r -> p h r u"))
+
+
+def regroup(copy, grouped, rows):
+    copy(
+        out=grouped.rearrange("p (c i) j -> p c j i", i=RUN),
+        in_=rows.rearrange("p j (c i) -> p c j i", i=RUN),
+    )
+
+
+def tile_memorymodule_pa_kernel(tc, q, mem, out):
+    nc = tc.nc
+    with ExitStack() as ctx:
+        keep = ctx.enter_context(tc.tile_pool(name="keep", bufs=1))
+        exps = ctx.enter_context(tc.tile_pool(name="exps", bufs=4))
+        results = ctx.enter_context(tc.tile_pool(name="results", bufs=SLOT_TILES * WIDTH_HALVES))
+        banks = ctx.enter_context(tc.psum_pool(name="banks", bufs=8))
+
+        identity = keep.tile([P, P], F32)
+        masks.make_identity(nc, identity[:])
+
+        zero = keep.tile([P, 1], F32)
+        one = keep.tile([P, 1], F32)
+        nc.vector.memset(zero[:], 0.0)
+        nc.scalar.activation(out=one[:], in_=zero[:], func=ACT.Exp)
+
+        mem_rows = keep.tile([P, SLOT_TILES * WIDTH], BF16)
+        mem_tiles = mem.rearrange("(i p) c -> i p c", p=P)
+        for i in range(SLOT_TILES):
+            nc.sync.dma_start(out=mem_rows[:, i * WIDTH : (i + 1) * WIDTH], in_=mem_tiles[i])
+        q_tiles = q.rearrange("(g p j) c -> g j p c", g=TOKEN_PASSES, j=PACK)
+        q_rows = []
+        for g in range(TOKEN_PASSES):
+            q_rows.append(keep.tile([P, PACK * WIDTH], BF16, name="q_rows%d" % g))
+            for j in range(PACK):
+                nc.sync.dma_start(out=q_rows[g][:, j * WIDTH : (j + 1) * WIDTH], in_=q_tiles[g, j])
+
+        mem_grouped = keep.tile([P, WIDTH_PASSES * SLOTS * PACK], BF16, align_bytes=64)
+        mem_codes = keep.tile([P, WIDTH_PASSES, SLOTS], U32, align_bytes=64)
+        mem_scales = keep.tile([P, WIDTH_PASSES, SLOTS], U8, align_bytes=64)
+        mem_words = mem_rows[:].bitcast(F32)
+        mem_grouped_words = mem_grouped[:].bitcast(F32).rearrange(
+            "p (h s u) -> p h s u", h=WIDTH_PASSES, u=PAIR
+        )
+        for i in range(SLOT_TILES):
+            flip_rows(
+                nc,
+                banks,
+                identity,
+                mem_words[:, i * WORDS : (i + 1) * WORDS],
+                mem_grouped_words[:, :, i * P : (i + 1) * P, :],
+                nc.scalar.copy,
+            )
+        for h in range(WIDTH_PASSES):
+            nc.vector.quantize_mx(
+                out=mem_codes[:, h, :].bitcast(FP8X4),
+                scales=mem_scales[:, h, :],
+                in_=mem_grouped[:, h * SLOTS * PACK : (h + 1) * SLOTS * PACK],
+            )
+
+        qw_grouped = keep.tile([P, TOKEN_TILES * WIDTH], BF16, align_bytes=64)
+        qw_codes = keep.tile([P, TOKEN_TILES, WIDTH_PASSES * P], U32, align_bytes=64)
+        qw_scales = keep.tile([P, TOKEN_TILES, WIDTH_PASSES * P], U8, align_bytes=64)
+        qw_grouped_words = qw_grouped[:].bitcast(F32).rearrange(
+            "p (k h r u) -> p k h r u", k=TOKEN_TILES, h=WIDTH_PASSES, u=PAIR
+        )
+        for k in range(TOKEN_TILES):
+            g, j = divmod(k, PACK)
+            flip_rows(
+                nc,
+                banks,
+                identity,
+                q_rows[g][:].bitcast(F32)[:, j * WORDS : (j + 1) * WORDS],
+                qw_grouped_words[:, k],
+                nc.scalar.copy,
+            )
+            nc.vector.quantize_mx(
+                out=qw_codes[:, k, :].bitcast(FP8X4),
+                scales=qw_scales[:, k, :],
+                in_=qw_grouped[:, k * WIDTH : (k + 1) * WIDTH],
+            )
+
+        qt_grouped = keep.tile([P, TOKEN_PASSES, WIDTH, PACK], BF16, align_bytes=64)
+        qt_codes = keep.tile([P, TOKEN_PASSES, WIDTH], U32, align_bytes=64)
+        qt_scales = keep.tile([P, TOKEN_PASSES, WIDTH], U8, align_bytes=64)
+        qt_copy = [nc.vector.tensor_copy, nc.scalar.copy]
+
+        def prepare_q_for_matmul_2(g, n):
+            columns = slice(n * N_BANK, (n + 1) * N_BANK)
+            rows = q_rows[g][:].rearrange("p (j c) -> p j c", j=PACK)
+            regroup(qt_copy[g], qt_grouped[:, g, columns, :], rows[:, :, columns])
+            nc.vector.quantize_mx(
+                out=qt_codes[:, g, columns].bitcast(FP8X4),
+                scales=qt_scales[:, g, columns],
+                in_=qt_grouped[:, g, columns, :].rearrange("p c j -> p (c j)"),
+            )
+
+        neg_max = keep.tile([P, TOKEN_TILES], F32)
+        totals = keep.tile([P, TOKEN_TILES], F32)
+        inverse = keep.tile([P, TOKEN_TILES], F32)
+        p_rows = keep.tile([P, TOKEN_PASSES, PACK, SLOTS], BF16)
+        p_grouped = keep.tile([P, TOKEN_PASSES, SLOTS, PACK], BF16, align_bytes=64)
+        p_codes = keep.tile([P, TOKEN_PASSES, SLOTS], U32, align_bytes=64)
+        p_scales = keep.tile([P, TOKEN_PASSES, SLOTS], U8, align_bytes=64)
+        p_copy = [nc.scalar.copy, nc.vector.tensor_copy]
+
+        for g in range(TOKEN_PASSES):
+            for j in range(PACK):
+                k = g * PACK + j
+                scores = banks.tile([P, SLOTS], F32, tag="bank")
+                for h in range(WIDTH_PASSES):
+                    tokens = slice(h * P, (h + 1) * P)
+                    nc.tensor.matmul_mx(
+                        out=scores[:],
+                        lhsT=qw_codes[:, k, tokens].bitcast(FP8X4),
+                        lhsT_scale=qw_scales[:, k, tokens],
+                        rhs=mem_codes[:, h, :].bitcast(FP8X4),
+                        rhs_scale=mem_scales[:, h, :],
+                        start=(h == 0),
+                        stop=(h == WIDTH_PASSES - 1),
+                    )
+                nc.vector.tensor_reduce(
+                    out=neg_max[:, k : k + 1], in_=scores[:], axis=AXIS.X, op=ALU.max, negate=True
+                )
+                exp_rows = exps.tile([P, SLOTS], F32)
+                nc.scalar.activation(
+                    out=exp_rows[:],
+                    in_=scores[:],
+                    func=ACT.Exp,
+                    bias=neg_max[:, k : k + 1],
+                    scale=1.0,
+                    accum_out=totals[:, k : k + 1],
+                )
+                nc.vector.reciprocal(out=inverse[:, k : k + 1], in_=totals[:, k : k + 1])
+                nc.vector.tensor_scalar(
+                    out=p_rows[:, g, j, :],
+                    in0=exp_rows[:],
+                    scalar1=inverse[:, k : k + 1],
+                    scalar2=FLOOR,
+                    op0=ALU.mult,
+                    op1=ALU.max,
+                )
+            regroup(p_copy[g], p_grouped[:, g], p_rows[:, g])
+            nc.vector.quantize_mx(
+                out=p_codes[:, g, :].bitcast(FP8X4),
+                scales=p_scales[:, g, :],
+                in_=p_grouped[:, g].rearrange("p s j -> p (s j)"),
+            )
+
+        out_copy = [nc.vector.tensor_copy, nc.scalar.copy]
+        for n in range(WIDTH_HALVES):
+            columns = slice(n * N_BANK, (n + 1) * N_BANK)
+            for g in range(TOKEN_PASSES):
+                prepare_q_for_matmul_2(g, n)
+            for i in range(SLOT_TILES):
+                slots = slice(i * P, (i + 1) * P)
+                sums = banks.tile([P, N_BANK], F32, tag="bank")
+                for g in range(TOKEN_PASSES):
+                    nc.tensor.matmul_mx(
+                        out=sums[:],
+                        lhsT=p_codes[:, g, slots].bitcast(FP8X4),
+                        lhsT_scale=p_scales[:, g, slots],
+                        rhs=qt_codes[:, g, columns].bitcast(FP8X4),
+                        rhs_scale=qt_scales[:, g, columns],
+                        start=(g == 0),
+                        stop=(g == TOKEN_PASSES - 1),
+                    )
+                result = results.tile([P, N_BANK], F32)
+                out_copy[i % 2](out=result[:], in_=sums[:])
+                nc.sync.dma_start(out=out[slots, columns], in_=result[:])

@@ -30,8 +30,19 @@ WIDTH_HALVES = WIDTH // N_BANK
 PAIR = 2
 WORDS = WIDTH // PAIR
 RUN = 4
+QUARTERS = 4
+LAG = 2
 
 FLOPS = 2 * 2 * TOKENS * WIDTH * SLOTS
+
+
+def half(n):
+    return slice(n * N_BANK, (n + 1) * N_BANK)
+
+
+def quarter(n, x):
+    width = N_BANK // QUARTERS
+    return slice(n * N_BANK + x * width, n * N_BANK + (x + 1) * width)
 
 
 def flip_rows(nc, banks, identity, row_words, grouped_words, copy):
@@ -54,9 +65,8 @@ def tile_memorymodule_pa_kernel(tc, q, mem, out):
     nc = tc.nc
     with ExitStack() as ctx:
         keep = ctx.enter_context(tc.tile_pool(name="keep", bufs=1))
-        exps = ctx.enter_context(tc.tile_pool(name="exps", bufs=4))
-        results = ctx.enter_context(tc.tile_pool(name="results", bufs=SLOT_TILES * WIDTH_HALVES))
         banks = ctx.enter_context(tc.psum_pool(name="banks", bufs=8))
+        ctx.enter_context(tc.manual_schedule())
 
         identity = keep.tile([P, P], F32)
         masks.make_identity(nc, identity[:])
@@ -66,47 +76,64 @@ def tile_memorymodule_pa_kernel(tc, q, mem, out):
         nc.vector.memset(zero[:], 0.0)
         nc.scalar.activation(out=one[:], in_=zero[:], func=ACT.Exp)
 
+        q_rows = [keep.tile([P, PACK * WIDTH], BF16, name="q_rows%d" % g) for g in range(TOKEN_PASSES)]
         mem_rows = keep.tile([P, SLOT_TILES * WIDTH], BF16)
-        mem_tiles = mem.rearrange("(i p) c -> i p c", p=P)
-        for i in range(SLOT_TILES):
-            nc.sync.dma_start(out=mem_rows[:, i * WIDTH : (i + 1) * WIDTH], in_=mem_tiles[i])
-        q_tiles = q.rearrange("(g p j) c -> g j p c", g=TOKEN_PASSES, j=PACK)
-        q_rows = []
-        for g in range(TOKEN_PASSES):
-            q_rows.append(keep.tile([P, PACK * WIDTH], BF16, name="q_rows%d" % g))
-            for j in range(PACK):
-                nc.sync.dma_start(out=q_rows[g][:, j * WIDTH : (j + 1) * WIDTH], in_=q_tiles[g, j])
-
         mem_grouped = keep.tile([P, WIDTH_PASSES * SLOTS * PACK], BF16, align_bytes=64)
         mem_codes = keep.tile([P, WIDTH_PASSES, SLOTS], U32, align_bytes=64)
         mem_scales = keep.tile([P, WIDTH_PASSES, SLOTS], U8, align_bytes=64)
-        mem_words = mem_rows[:].bitcast(F32)
+        qw_grouped = keep.tile([P, TOKEN_TILES * WIDTH], BF16, align_bytes=64)
+        qw_codes = keep.tile([P, TOKEN_TILES, WIDTH_PASSES * P], U32, align_bytes=64)
+        qw_scales = keep.tile([P, TOKEN_TILES, WIDTH_PASSES * P], U8, align_bytes=64)
+        qt_grouped = keep.tile([P, TOKEN_PASSES, WIDTH, PACK], BF16, align_bytes=64)
+        qt_codes = keep.tile([P, TOKEN_PASSES, WIDTH], U32, align_bytes=64)
+        qt_scales = keep.tile([P, TOKEN_PASSES, WIDTH], U8, align_bytes=64)
+        neg_max = keep.tile([P, TOKEN_TILES], F32)
+        totals = keep.tile([P, TOKEN_TILES], F32)
+        inverse = keep.tile([P, TOKEN_TILES], F32)
+        exp_rows = keep.tile([P, TOKEN_TILES, SLOTS], F32)
+        p_rows = keep.tile([P, TOKEN_PASSES, PACK, SLOTS], BF16)
+        p_grouped = keep.tile([P, TOKEN_PASSES, SLOTS, PACK], BF16, align_bytes=64)
+        p_codes = keep.tile([P, TOKEN_PASSES, SLOTS], U32, align_bytes=64)
+        p_scales = keep.tile([P, TOKEN_PASSES, SLOTS], U8, align_bytes=64)
+        results = keep.tile([P, SLOT_TILES, WIDTH], F32)
+
+        q_tiles = q.rearrange("(g p j) c -> g j p c", g=TOKEN_PASSES, j=PACK)
+        mem_tiles = mem.rearrange("(i p) c -> i p c", p=P)
+
+        def load_q(g):
+            for j in range(PACK):
+                nc.sync.dma_start(out=q_rows[g][:, j * WIDTH : (j + 1) * WIDTH], in_=q_tiles[g, j])
+
+        load_q(0)
+        for i in range(SLOT_TILES):
+            nc.sync.dma_start(out=mem_rows[:, i * WIDTH : (i + 1) * WIDTH], in_=mem_tiles[i])
+        load_q(1)
+
         mem_grouped_words = mem_grouped[:].bitcast(F32).rearrange(
             "p (h s u) -> p h s u", h=WIDTH_PASSES, u=PAIR
         )
-        for i in range(SLOT_TILES):
+        qw_grouped_words = qw_grouped[:].bitcast(F32).rearrange(
+            "p (k h r u) -> p k h r u", k=TOKEN_TILES, h=WIDTH_PASSES, u=PAIR
+        )
+
+        def flip_mem(i):
             flip_rows(
                 nc,
                 banks,
                 identity,
-                mem_words[:, i * WORDS : (i + 1) * WORDS],
+                mem_rows[:].bitcast(F32)[:, i * WORDS : (i + 1) * WORDS],
                 mem_grouped_words[:, :, i * P : (i + 1) * P, :],
                 nc.scalar.copy,
             )
-        for h in range(WIDTH_PASSES):
+
+        def quantise_mem(h):
             nc.vector.quantize_mx(
                 out=mem_codes[:, h, :].bitcast(FP8X4),
                 scales=mem_scales[:, h, :],
                 in_=mem_grouped[:, h * SLOTS * PACK : (h + 1) * SLOTS * PACK],
             )
 
-        qw_grouped = keep.tile([P, TOKEN_TILES * WIDTH], BF16, align_bytes=64)
-        qw_codes = keep.tile([P, TOKEN_TILES, WIDTH_PASSES * P], U32, align_bytes=64)
-        qw_scales = keep.tile([P, TOKEN_TILES, WIDTH_PASSES * P], U8, align_bytes=64)
-        qw_grouped_words = qw_grouped[:].bitcast(F32).rearrange(
-            "p (k h r u) -> p k h r u", k=TOKEN_TILES, h=WIDTH_PASSES, u=PAIR
-        )
-        for k in range(TOKEN_TILES):
+        def flip_q(k):
             g, j = divmod(k, PACK)
             flip_rows(
                 nc,
@@ -116,97 +143,122 @@ def tile_memorymodule_pa_kernel(tc, q, mem, out):
                 qw_grouped_words[:, k],
                 nc.scalar.copy,
             )
+
+        def quantise_q_along_width(k):
             nc.vector.quantize_mx(
                 out=qw_codes[:, k, :].bitcast(FP8X4),
                 scales=qw_scales[:, k, :],
                 in_=qw_grouped[:, k * WIDTH : (k + 1) * WIDTH],
             )
 
-        qt_grouped = keep.tile([P, TOKEN_PASSES, WIDTH, PACK], BF16, align_bytes=64)
-        qt_codes = keep.tile([P, TOKEN_PASSES, WIDTH], U32, align_bytes=64)
-        qt_scales = keep.tile([P, TOKEN_PASSES, WIDTH], U8, align_bytes=64)
-        qt_copy = [nc.vector.tensor_copy, nc.scalar.copy]
-
-        def prepare_q_for_matmul_2(g, n):
-            columns = slice(n * N_BANK, (n + 1) * N_BANK)
+        def regroup_q(copy, g, columns):
             rows = q_rows[g][:].rearrange("p (j c) -> p j c", j=PACK)
-            regroup(qt_copy[g], qt_grouped[:, g, columns, :], rows[:, :, columns])
+            regroup(copy, qt_grouped[:, g, columns, :], rows[:, :, columns])
+
+        def quantise_q_along_tokens(g, n):
             nc.vector.quantize_mx(
-                out=qt_codes[:, g, columns].bitcast(FP8X4),
-                scales=qt_scales[:, g, columns],
-                in_=qt_grouped[:, g, columns, :].rearrange("p c j -> p (c j)"),
+                out=qt_codes[:, g, half(n)].bitcast(FP8X4),
+                scales=qt_scales[:, g, half(n)],
+                in_=qt_grouped[:, g, half(n), :].rearrange("p c j -> p (c j)"),
             )
 
-        neg_max = keep.tile([P, TOKEN_TILES], F32)
-        totals = keep.tile([P, TOKEN_TILES], F32)
-        inverse = keep.tile([P, TOKEN_TILES], F32)
-        p_rows = keep.tile([P, TOKEN_PASSES, PACK, SLOTS], BF16)
-        p_grouped = keep.tile([P, TOKEN_PASSES, SLOTS, PACK], BF16, align_bytes=64)
-        p_codes = keep.tile([P, TOKEN_PASSES, SLOTS], U32, align_bytes=64)
-        p_scales = keep.tile([P, TOKEN_PASSES, SLOTS], U8, align_bytes=64)
-        p_copy = [nc.scalar.copy, nc.vector.tensor_copy]
+        def scores_and_maximum(k):
+            scores = banks.tile([P, SLOTS], F32, tag="bank")
+            for h in range(WIDTH_PASSES):
+                tokens = slice(h * P, (h + 1) * P)
+                nc.tensor.matmul_mx(
+                    out=scores[:],
+                    lhsT=qw_codes[:, k, tokens].bitcast(FP8X4),
+                    lhsT_scale=qw_scales[:, k, tokens],
+                    rhs=mem_codes[:, h, :].bitcast(FP8X4),
+                    rhs_scale=mem_scales[:, h, :],
+                    start=(h == 0),
+                    stop=(h == WIDTH_PASSES - 1),
+                )
+            nc.vector.tensor_reduce(
+                out=neg_max[:, k : k + 1], in_=scores[:], axis=AXIS.X, op=ALU.max, negate=True
+            )
+            return scores
 
-        for g in range(TOKEN_PASSES):
-            for j in range(PACK):
-                k = g * PACK + j
-                scores = banks.tile([P, SLOTS], F32, tag="bank")
-                for h in range(WIDTH_PASSES):
-                    tokens = slice(h * P, (h + 1) * P)
-                    nc.tensor.matmul_mx(
-                        out=scores[:],
-                        lhsT=qw_codes[:, k, tokens].bitcast(FP8X4),
-                        lhsT_scale=qw_scales[:, k, tokens],
-                        rhs=mem_codes[:, h, :].bitcast(FP8X4),
-                        rhs_scale=mem_scales[:, h, :],
-                        start=(h == 0),
-                        stop=(h == WIDTH_PASSES - 1),
-                    )
-                nc.vector.tensor_reduce(
-                    out=neg_max[:, k : k + 1], in_=scores[:], axis=AXIS.X, op=ALU.max, negate=True
-                )
-                exp_rows = exps.tile([P, SLOTS], F32)
-                nc.scalar.activation(
-                    out=exp_rows[:],
-                    in_=scores[:],
-                    func=ACT.Exp,
-                    bias=neg_max[:, k : k + 1],
-                    scale=1.0,
-                    accum_out=totals[:, k : k + 1],
-                )
-                nc.vector.reciprocal(out=inverse[:, k : k + 1], in_=totals[:, k : k + 1])
-                nc.vector.tensor_scalar(
-                    out=p_rows[:, g, j, :],
-                    in0=exp_rows[:],
-                    scalar1=inverse[:, k : k + 1],
-                    scalar2=FLOOR,
-                    op0=ALU.mult,
-                    op1=ALU.max,
-                )
-            regroup(p_copy[g], p_grouped[:, g], p_rows[:, g])
+        def exponential(k, scores):
+            nc.scalar.activation(
+                out=exp_rows[:, k, :],
+                in_=scores[:],
+                func=ACT.Exp,
+                bias=neg_max[:, k : k + 1],
+                scale=1.0,
+                accum_out=totals[:, k : k + 1],
+            )
+
+        def normalise(k):
+            g, j = divmod(k, PACK)
+            nc.vector.reciprocal(out=inverse[:, k : k + 1], in_=totals[:, k : k + 1])
+            nc.vector.tensor_scalar(
+                out=p_rows[:, g, j, :],
+                in0=exp_rows[:, k, :],
+                scalar1=inverse[:, k : k + 1],
+                scalar2=FLOOR,
+                op0=ALU.mult,
+                op1=ALU.max,
+            )
+
+        def quantise_p(g):
             nc.vector.quantize_mx(
                 out=p_codes[:, g, :].bitcast(FP8X4),
                 scales=p_scales[:, g, :],
                 in_=p_grouped[:, g].rearrange("p s j -> p (s j)"),
             )
 
-        out_copy = [nc.vector.tensor_copy, nc.scalar.copy]
-        for n in range(WIDTH_HALVES):
-            columns = slice(n * N_BANK, (n + 1) * N_BANK)
+        def matmul_2(i, n, copy):
+            slots = slice(i * P, (i + 1) * P)
+            sums = banks.tile([P, N_BANK], F32, tag="bank")
             for g in range(TOKEN_PASSES):
-                prepare_q_for_matmul_2(g, n)
-            for i in range(SLOT_TILES):
-                slots = slice(i * P, (i + 1) * P)
-                sums = banks.tile([P, N_BANK], F32, tag="bank")
-                for g in range(TOKEN_PASSES):
-                    nc.tensor.matmul_mx(
-                        out=sums[:],
-                        lhsT=p_codes[:, g, slots].bitcast(FP8X4),
-                        lhsT_scale=p_scales[:, g, slots],
-                        rhs=qt_codes[:, g, columns].bitcast(FP8X4),
-                        rhs_scale=qt_scales[:, g, columns],
-                        start=(g == 0),
-                        stop=(g == TOKEN_PASSES - 1),
-                    )
-                result = results.tile([P, N_BANK], F32)
-                out_copy[i % 2](out=result[:], in_=sums[:])
-                nc.sync.dma_start(out=out[slots, columns], in_=result[:])
+                nc.tensor.matmul_mx(
+                    out=sums[:],
+                    lhsT=p_codes[:, g, slots].bitcast(FP8X4),
+                    lhsT_scale=p_scales[:, g, slots],
+                    rhs=qt_codes[:, g, half(n)].bitcast(FP8X4),
+                    rhs_scale=qt_scales[:, g, half(n)],
+                    start=(g == 0),
+                    stop=(g == TOKEN_PASSES - 1),
+                )
+            copy(out=results[:, i, half(n)], in_=sums[:])
+            nc.sync.dma_start(out=out[slots, half(n)], in_=results[:, i, half(n)])
+
+        for k in range(PACK):
+            flip_q(k)
+            quantise_q_along_width(k)
+            regroup_q(nc.vector.tensor_copy, 0, quarter(0, k))
+        quantise_q_along_tokens(0, 0)
+        regroup_q(nc.vector.tensor_copy, 0, half(1))
+        for i in range(SLOT_TILES):
+            flip_mem(i)
+        for h in range(WIDTH_PASSES):
+            quantise_mem(h)
+        for k in range(PACK, TOKEN_TILES):
+            flip_q(k)
+            quantise_q_along_width(k)
+
+        for k in range(TOKEN_TILES):
+            scores = scores_and_maximum(k)
+            if k < QUARTERS:
+                regroup_q(nc.scalar.copy, 1, quarter(0, k))
+            exponential(k, scores)
+            if k >= LAG:
+                normalise(k - LAG)
+        quantise_q_along_tokens(1, 0)
+        for k in range(TOKEN_TILES - LAG, TOKEN_TILES):
+            normalise(k)
+
+        regroup(nc.scalar.copy, p_grouped[:, 0], p_rows[:, 0])
+        regroup(nc.vector.tensor_copy, p_grouped[:, 1], p_rows[:, 1])
+        for g in range(TOKEN_PASSES):
+            quantise_p(g)
+
+        regroup_q(nc.scalar.copy, 1, half(1))
+        for g in range(TOKEN_PASSES):
+            quantise_q_along_tokens(g, 1)
+        for i in range(SLOT_TILES):
+            matmul_2(i, 0, nc.scalar.copy)
+        for i in range(SLOT_TILES):
+            matmul_2(i, 1, [nc.scalar.copy, nc.vector.tensor_copy][i % 2])

@@ -190,9 +190,11 @@ def tile_memorymodule_pa_kernel(tc, q, mem, out):
                 accum_out=totals[:, k : k + 1],
             )
 
-        def normalise(k):
-            g, j = divmod(k, PACK)
+        def reciprocal(k):
             nc.vector.reciprocal(out=inverse[:, k : k + 1], in_=totals[:, k : k + 1])
+
+        def scale_and_floor(k):
+            g, j = divmod(k, PACK)
             nc.vector.tensor_scalar(
                 out=p_rows[:, g, j, :],
                 in0=exp_rows[:, k, :],
@@ -202,63 +204,94 @@ def tile_memorymodule_pa_kernel(tc, q, mem, out):
                 op1=ALU.max,
             )
 
-        def quantise_p(g):
+        def regroup_p(copy, g, i):
+            slots = slice(i * P, (i + 1) * P)
+            regroup(copy, p_grouped[:, g, slots, :], p_rows[:, g, :, slots])
+
+        def quantise_p(g, i):
+            slots = slice(i * P, (i + 1) * P)
             nc.vector.quantize_mx(
-                out=p_codes[:, g, :].bitcast(FP8X4),
-                scales=p_scales[:, g, :],
-                in_=p_grouped[:, g].rearrange("p s j -> p (s j)"),
+                out=p_codes[:, g, slots].bitcast(FP8X4),
+                scales=p_scales[:, g, slots],
+                in_=p_grouped[:, g, slots, :].rearrange("p s j -> p (s j)"),
             )
 
-        def matmul_2(i, n, copy):
+        sums = {}
+
+        def matmul_2_pass(i, n, g):
             slots = slice(i * P, (i + 1) * P)
-            sums = banks.tile([P, N_BANK], F32, tag="bank")
-            for g in range(TOKEN_PASSES):
-                nc.tensor.matmul_mx(
-                    out=sums[:],
-                    lhsT=p_codes[:, g, slots].bitcast(FP8X4),
-                    lhsT_scale=p_scales[:, g, slots],
-                    rhs=qt_codes[:, g, half(n)].bitcast(FP8X4),
-                    rhs_scale=qt_scales[:, g, half(n)],
-                    start=(g == 0),
-                    stop=(g == TOKEN_PASSES - 1),
-                )
-            copy(out=results[:, i, half(n)], in_=sums[:])
+            nc.tensor.matmul_mx(
+                out=sums[(i, n)][:],
+                lhsT=p_codes[:, g, slots].bitcast(FP8X4),
+                lhsT_scale=p_scales[:, g, slots],
+                rhs=qt_codes[:, g, half(n)].bitcast(FP8X4),
+                rhs_scale=qt_scales[:, g, half(n)],
+                start=(g == 0),
+                stop=(g == TOKEN_PASSES - 1),
+            )
+
+        def first_pass(i, n):
+            sums[(i, n)] = banks.tile([P, N_BANK], F32, tag="bank", name="sums%d%d" % (i, n))
+            matmul_2_pass(i, n, 0)
+
+        def last_pass_and_store(i, n, copy):
+            slots = slice(i * P, (i + 1) * P)
+            matmul_2_pass(i, n, 1)
+            copy(out=results[:, i, half(n)], in_=sums[(i, n)][:])
             nc.sync.dma_start(out=out[slots, half(n)], in_=results[:, i, half(n)])
 
         for k in range(PACK):
             flip_q(k)
             quantise_q_along_width(k)
             regroup_q(nc.vector.tensor_copy, 0, quarter(0, k))
-        quantise_q_along_tokens(0, 0)
         regroup_q(nc.vector.tensor_copy, 0, half(1))
+        quantise_q_along_tokens(0, 0)
         for i in range(SLOT_TILES):
             flip_mem(i)
         for h in range(WIDTH_PASSES):
             quantise_mem(h)
+        quantise_q_along_tokens(0, 1)
         for k in range(PACK, TOKEN_TILES):
             flip_q(k)
             quantise_q_along_width(k)
 
         for k in range(TOKEN_TILES):
+            if k >= LAG:
+                reciprocal(k - LAG)
             scores = scores_and_maximum(k)
             if k < QUARTERS:
                 regroup_q(nc.scalar.copy, 1, quarter(0, k))
             exponential(k, scores)
             if k >= LAG:
-                normalise(k - LAG)
+                scale_and_floor(k - LAG)
+
+        for i in range(SLOT_TILES):
+            regroup_p(nc.scalar.copy, 0, i)
+        assert LAG == 2
+        reciprocal(TOKEN_TILES - 2)
         quantise_q_along_tokens(1, 0)
-        for k in range(TOKEN_TILES - LAG, TOKEN_TILES):
-            normalise(k)
-
-        regroup(nc.scalar.copy, p_grouped[:, 0], p_rows[:, 0])
-        regroup(nc.vector.tensor_copy, p_grouped[:, 1], p_rows[:, 1])
-        for g in range(TOKEN_PASSES):
-            quantise_p(g)
-
-        regroup_q(nc.scalar.copy, 1, half(1))
-        for g in range(TOKEN_PASSES):
-            quantise_q_along_tokens(g, 1)
+        scale_and_floor(TOKEN_TILES - 2)
+        reciprocal(TOKEN_TILES - 1)
+        quantise_p(0, 0)
+        scale_and_floor(TOKEN_TILES - 1)
         for i in range(SLOT_TILES):
-            matmul_2(i, 0, nc.scalar.copy)
+            if i + 1 < SLOT_TILES:
+                quantise_p(0, i + 1)
+            regroup_p(nc.vector.tensor_copy, 1, i)
+            if i >= 1:
+                quantise_p(1, i - 1)
+        quantise_p(1, SLOT_TILES - 1)
+
+        for x in range(QUARTERS):
+            regroup_q([nc.scalar.copy, nc.vector.tensor_copy][x // 2], 1, quarter(1, x))
+        quantise_q_along_tokens(1, 1)
+
+        first_pass(0, 0)
         for i in range(SLOT_TILES):
-            matmul_2(i, 1, [nc.scalar.copy, nc.vector.tensor_copy][i % 2])
+            if i + 1 < SLOT_TILES:
+                first_pass(i + 1, 0)
+            last_pass_and_store(i, 0, nc.scalar.copy)
+        for i in range(SLOT_TILES):
+            first_pass(i, 1)
+        for i in range(SLOT_TILES):
+            last_pass_and_store(i, 1, [nc.scalar.copy, nc.vector.tensor_copy][i % 2])

@@ -30,7 +30,6 @@ WIDTH_HALVES = WIDTH // N_BANK
 PAIR = 2
 WORDS = WIDTH // PAIR
 RUN = 4
-QUARTERS = 4
 LAG = 2
 
 FLOPS = 2 * 2 * TOKENS * WIDTH * SLOTS
@@ -40,18 +39,17 @@ def half(n):
     return slice(n * N_BANK, (n + 1) * N_BANK)
 
 
-def quarter(n, x):
-    width = N_BANK // QUARTERS
+def piece(n, x, parts):
+    width = N_BANK // parts
     return slice(n * N_BANK + x * width, n * N_BANK + (x + 1) * width)
 
 
-def flip_rows(nc, banks, identity, row_words, grouped_words, copy):
-    flipped = banks.tile([P, WIDTH_PASSES, PAIR, P], F32, tag="bank")
-    for h in range(WIDTH_PASSES):
+def flip_rows(nc, banks, identity, blocks, grouped_words, copy):
+    flipped = banks.tile([P, 2, PAIR, P], F32, tag="bank")
+    for b in range(2):
         for u in range(PAIR):
-            first = (h * PAIR + u) * P
-            nc.tensor.transpose(flipped[:, h, u, :], row_words[:, first : first + P], identity[:])
-    copy(out=grouped_words, in_=flipped[:].rearrange("p h u r -> p h r u"))
+            nc.tensor.transpose(flipped[:, b, u, :], blocks[b][u], identity[:])
+    copy(out=grouped_words, in_=flipped[:].rearrange("p b u r -> p b r u"))
 
 
 def regroup(copy, grouped, rows):
@@ -71,19 +69,23 @@ def tile_memorymodule_pa_kernel(tc, q, mem, out):
         identity = keep.tile([P, P], F32)
         masks.make_identity(nc, identity[:])
 
+        identity_bf16 = keep.tile([P, P], BF16)
+        masks.make_identity(nc, identity_bf16[:])
+
         zero = keep.tile([P, 1], F32)
         one = keep.tile([P, 1], F32)
         nc.vector.memset(zero[:], 0.0)
         nc.scalar.activation(out=one[:], in_=zero[:], func=ACT.Exp)
 
-        q_rows = [keep.tile([P, PACK * WIDTH], BF16, name="q_rows%d" % g) for g in range(TOKEN_PASSES)]
+        q_halves = [keep.tile([P, PACK, N_BANK], BF16, name="q_half%d" % h) for h in range(WIDTH_HALVES)]
+        q_last = keep.tile([P, PACK, WIDTH], BF16)
         mem_rows = keep.tile([P, SLOT_TILES * WIDTH], BF16)
         mem_grouped = keep.tile([P, WIDTH_PASSES * SLOTS * PACK], BF16, align_bytes=64)
         mem_codes = keep.tile([P, WIDTH_PASSES, SLOTS], U32, align_bytes=64)
         mem_scales = keep.tile([P, WIDTH_PASSES, SLOTS], U8, align_bytes=64)
-        qw_grouped = keep.tile([P, TOKEN_TILES * WIDTH], BF16, align_bytes=64)
-        qw_codes = keep.tile([P, TOKEN_TILES, WIDTH_PASSES * P], U32, align_bytes=64)
-        qw_scales = keep.tile([P, TOKEN_TILES, WIDTH_PASSES * P], U8, align_bytes=64)
+        qw_grouped = keep.tile([P, WIDTH_PASSES * TOKENS * PACK], BF16, align_bytes=64)
+        qw_codes = keep.tile([P, WIDTH_PASSES, TOKENS], U32, align_bytes=64)
+        qw_scales = keep.tile([P, WIDTH_PASSES, TOKENS], U8, align_bytes=64)
         qt_grouped = keep.tile([P, TOKEN_PASSES, WIDTH, PACK], BF16, align_bytes=64)
         qt_codes = keep.tile([P, TOKEN_PASSES, WIDTH], U32, align_bytes=64)
         qt_scales = keep.tile([P, TOKEN_PASSES, WIDTH], U8, align_bytes=64)
@@ -97,34 +99,45 @@ def tile_memorymodule_pa_kernel(tc, q, mem, out):
         p_scales = keep.tile([P, TOKEN_PASSES, SLOTS], U8, align_bytes=64)
         results = keep.tile([P, SLOT_TILES, WIDTH], F32)
 
-        q_tiles = q.rearrange("(g p j) c -> g j p c", g=TOKEN_PASSES, j=PACK)
-        mem_tiles = mem.rearrange("(i p) c -> i p c", p=P)
+        q_view = q.rearrange("(g p j) c -> g p j c", g=TOKEN_PASSES, j=PACK)
+        mem_view = mem.rearrange("(p i) c -> p i c", i=SLOT_TILES)
+        out_tiles = out.rearrange("(p i) c -> i p c", i=SLOT_TILES)
+        mem_rows_view = mem_rows[:].rearrange("p (i c) -> p i c", i=SLOT_TILES)
 
-        def load_q(g):
-            for j in range(PACK):
-                nc.sync.dma_start(out=q_rows[g][:, j * WIDTH : (j + 1) * WIDTH], in_=q_tiles[g, j])
-
-        load_q(0)
-        for i in range(SLOT_TILES):
-            nc.sync.dma_start(out=mem_rows[:, i * WIDTH : (i + 1) * WIDTH], in_=mem_tiles[i])
-        load_q(1)
+        for h in range(WIDTH_PASSES):
+            for first in range(0, PACK, 2):
+                pair = slice(first, first + 2)
+                nc.sync.dma_start(out=q_halves[h][:, pair, :], in_=q_view[0][:, pair, half(h)])
+        for first in range(0, SLOT_TILES, 2):
+            pair = slice(first, first + 2)
+            nc.sync.dma_start(out=mem_rows_view[:, pair, :], in_=mem_view[:, pair, :])
+        for first in range(0, PACK, 2):
+            pair = slice(first, first + 2)
+            nc.sync.dma_start(out=q_last[:, pair, :], in_=q_view[1][:, pair, :])
 
         mem_grouped_words = mem_grouped[:].bitcast(F32).rearrange(
             "p (h s u) -> p h s u", h=WIDTH_PASSES, u=PAIR
         )
         qw_grouped_words = qw_grouped[:].bitcast(F32).rearrange(
-            "p (k h r u) -> p k h r u", k=TOKEN_TILES, h=WIDTH_PASSES, u=PAIR
+            "p (h k r u) -> p h k r u", h=WIDTH_PASSES, k=TOKEN_TILES, u=PAIR
         )
 
-        def flip_mem(i):
-            flip_rows(
-                nc,
-                banks,
-                identity,
-                mem_rows[:].bitcast(F32)[:, i * WORDS : (i + 1) * WORDS],
-                mem_grouped_words[:, :, i * P : (i + 1) * P, :],
-                nc.scalar.copy,
-            )
+        def words_of(rows):
+            words = rows.bitcast(F32)
+            return [words[:, u * P : (u + 1) * P] for u in range(PAIR)]
+
+        def q_columns(g, columns):
+            if g == 0:
+                h, first = divmod(columns.start, N_BANK)
+                return q_halves[h][:, :, first : first + columns.stop - columns.start]
+            return q_last[:, :, columns]
+
+
+        def flip_two_mem_tiles(i, h, copy):
+            slots = slice(i * P, (i + 2) * P)
+            blocks = [words_of(mem_rows_view[:, i + b, half(h)]) for b in range(2)]
+            grouped = mem_grouped_words[:, h, slots, :].rearrange("p (b r) u -> p b r u", b=2)
+            flip_rows(nc, banks, identity, blocks, grouped, copy)
 
         def quantise_mem(h):
             nc.vector.quantize_mx(
@@ -133,27 +146,37 @@ def tile_memorymodule_pa_kernel(tc, q, mem, out):
                 in_=mem_grouped[:, h * SLOTS * PACK : (h + 1) * SLOTS * PACK],
             )
 
-        def flip_q(k):
+        def flip_two_tiles(k, h, copy):
             g, j = divmod(k, PACK)
-            flip_rows(
-                nc,
-                banks,
-                identity,
-                q_rows[g][:].bitcast(F32)[:, j * WORDS : (j + 1) * WORDS],
-                qw_grouped_words[:, k],
-                nc.scalar.copy,
-            )
+            blocks = [words_of(q_columns(g, half(h))[:, j + b, :]) for b in range(2)]
+            flip_rows(nc, banks, identity, blocks, qw_grouped_words[:, h, k : k + 2], copy)
 
-        def quantise_q_along_width(k):
+        def quantise_q_along_width(k, h):
+            tokens = slice(k * P, (k + 2) * P)
+            first = h * TOKENS + k * P
             nc.vector.quantize_mx(
-                out=qw_codes[:, k, :].bitcast(FP8X4),
-                scales=qw_scales[:, k, :],
-                in_=qw_grouped[:, k * WIDTH : (k + 1) * WIDTH],
+                out=qw_codes[:, h, tokens].bitcast(FP8X4),
+                scales=qw_scales[:, h, tokens],
+                in_=qw_grouped[:, first * PACK : (first + 2 * P) * PACK],
             )
 
         def regroup_q(copy, g, columns):
-            rows = q_rows[g][:].rearrange("p (j c) -> p j c", j=PACK)
-            regroup(copy, qt_grouped[:, g, columns, :], rows[:, :, columns])
+            regroup(copy, qt_grouped[:, g, columns, :], q_columns(g, columns))
+
+        def spread_q(copy, g, x):
+            columns = slice(x * 256, (x + 1) * 256)
+            spread = banks.tile([P, 256, PACK], BF16, tag="bank")
+            rows = q_columns(g, columns)
+            for y in range(2):
+                part = slice(y * 128, (y + 1) * 128)
+                nc.tensor.matmul(
+                    out=spread[:, part, :],
+                    lhsT=identity_bf16[:],
+                    rhs=rows[:, :, part].rearrange("p j c -> p c j"),
+                    start=True,
+                    stop=True,
+                )
+            copy(out=qt_grouped[:, g, columns, :], in_=spread[:])
 
         def quantise_q_along_tokens(g, n):
             nc.vector.quantize_mx(
@@ -162,28 +185,32 @@ def tile_memorymodule_pa_kernel(tc, q, mem, out):
                 in_=qt_grouped[:, g, half(n), :].rearrange("p c j -> p (c j)"),
             )
 
-        def scores_and_maximum(k):
+        score_banks = {}
+
+        def multiply_scores(k):
+            tokens = slice(k * P, (k + 1) * P)
             scores = banks.tile([P, SLOTS], F32, tag="bank")
             for h in range(WIDTH_PASSES):
-                tokens = slice(h * P, (h + 1) * P)
                 nc.tensor.matmul_mx(
                     out=scores[:],
-                    lhsT=qw_codes[:, k, tokens].bitcast(FP8X4),
-                    lhsT_scale=qw_scales[:, k, tokens],
+                    lhsT=qw_codes[:, h, tokens].bitcast(FP8X4),
+                    lhsT_scale=qw_scales[:, h, tokens],
                     rhs=mem_codes[:, h, :].bitcast(FP8X4),
                     rhs_scale=mem_scales[:, h, :],
                     start=(h == 0),
                     stop=(h == WIDTH_PASSES - 1),
                 )
-            nc.vector.tensor_reduce(
-                out=neg_max[:, k : k + 1], in_=scores[:], axis=AXIS.X, op=ALU.max, negate=True
-            )
-            return scores
+            score_banks[k] = scores
 
-        def exponential(k, scores):
+        def maximum(k):
+            nc.vector.tensor_reduce(
+                out=neg_max[:, k : k + 1], in_=score_banks[k][:], axis=AXIS.X, op=ALU.max, negate=True
+            )
+
+        def exponential(k):
             nc.scalar.activation(
                 out=exp_rows[:, k, :],
-                in_=scores[:],
+                in_=score_banks[k][:],
                 func=ACT.Exp,
                 bias=neg_max[:, k : k + 1],
                 scale=1.0,
@@ -193,9 +220,9 @@ def tile_memorymodule_pa_kernel(tc, q, mem, out):
         def reciprocal(k):
             nc.vector.reciprocal(out=inverse[:, k : k + 1], in_=totals[:, k : k + 1])
 
-        def scale_and_floor(k):
+        def scale_and_floor(engine, k):
             g, j = divmod(k, PACK)
-            nc.vector.tensor_scalar(
+            engine.tensor_scalar(
                 out=p_rows[:, g, j, :],
                 in0=exp_rows[:, k, :],
                 scalar1=inverse[:, k : k + 1],
@@ -207,6 +234,21 @@ def tile_memorymodule_pa_kernel(tc, q, mem, out):
         def regroup_p(copy, g, i):
             slots = slice(i * P, (i + 1) * P)
             regroup(copy, p_grouped[:, g, slots, :], p_rows[:, g, :, slots])
+
+        def spread_p(copy, g, x):
+            slots = slice(x * 256, (x + 1) * 256)
+            spread = banks.tile([P, 256, PACK], BF16, tag="bank")
+            for y in range(2):
+                part = slice(y * 128, (y + 1) * 128)
+                rows = p_rows[:, g, :, slots][:, :, part]
+                nc.tensor.matmul(
+                    out=spread[:, part, :],
+                    lhsT=identity_bf16[:],
+                    rhs=rows.rearrange("p j s -> p s j"),
+                    start=True,
+                    stop=True,
+                )
+            copy(out=p_grouped[:, g, slots, :], in_=spread[:])
 
         def quantise_p(g, i):
             slots = slice(i * P, (i + 1) * P)
@@ -235,63 +277,86 @@ def tile_memorymodule_pa_kernel(tc, q, mem, out):
             matmul_2_pass(i, n, 0)
 
         def last_pass_and_store(i, n, copy):
-            slots = slice(i * P, (i + 1) * P)
             matmul_2_pass(i, n, 1)
             copy(out=results[:, i, half(n)], in_=sums[(i, n)][:])
-            nc.sync.dma_start(out=out[slots, half(n)], in_=results[:, i, half(n)])
+            nc.sync.dma_start(out=out_tiles[i][:, half(n)], in_=results[:, i, half(n)])
 
-        for k in range(PACK):
-            flip_q(k)
-            quantise_q_along_width(k)
-            regroup_q(nc.vector.tensor_copy, 0, quarter(0, k))
-        regroup_q(nc.vector.tensor_copy, 0, half(1))
+        on_scalar, on_vector = nc.scalar.copy, nc.vector.tensor_copy
+        flip_two_tiles(0, 0, on_scalar)
+        flip_two_tiles(2, 0, on_scalar)
+        regroup_q(on_vector, 0, piece(0, 0, 2))
+        quantise_q_along_width(0, 0)
+        regroup_q(on_vector, 0, piece(0, 1, 2))
+        flip_two_tiles(0, 1, on_scalar)
+        flip_two_tiles(2, 1, on_scalar)
+        quantise_q_along_width(2, 0)
         quantise_q_along_tokens(0, 0)
-        for i in range(SLOT_TILES):
-            flip_mem(i)
-        for h in range(WIDTH_PASSES):
-            quantise_mem(h)
+        quantise_q_along_width(0, 1)
+        regroup_q(on_scalar, 0, piece(1, 3, 4))
+        regroup_q(on_vector, 0, piece(1, 0, 2))
+        regroup_q(on_vector, 0, piece(1, 2, 4))
+        quantise_q_along_width(2, 1)
+        for i in (0, 2):
+            for h in range(WIDTH_PASSES):
+                flip_two_mem_tiles(i, h, on_scalar)
         quantise_q_along_tokens(0, 1)
-        for k in range(PACK, TOKEN_TILES):
-            flip_q(k)
-            quantise_q_along_width(k)
+        flip_two_tiles(4, 0, on_scalar)
+        flip_two_tiles(4, 1, on_scalar)
+        quantise_mem(0)
+        quantise_mem(1)
+        multiply_scores(0)
+        regroup_q(on_scalar, 1, piece(0, 0, 4))
+        flip_two_tiles(6, 0, on_scalar)
+        flip_two_tiles(6, 1, on_scalar)
+        quantise_q_along_width(4, 0)
+        regroup_q(on_vector, 1, piece(0, 1, 4))
+        quantise_q_along_width(4, 1)
 
+        spread = {0: 1, 2: 2, 4: 3}
         for k in range(TOKEN_TILES):
             if k >= LAG:
                 reciprocal(k - LAG)
-            scores = scores_and_maximum(k)
-            if k < QUARTERS:
-                regroup_q(nc.scalar.copy, 1, quarter(0, k))
-            exponential(k, scores)
+            maximum(k)
+            if k == 0:
+                quantise_q_along_width(6, 0)
+                quantise_q_along_width(6, 1)
+            exponential(k)
+            if k + 1 < TOKEN_TILES:
+                multiply_scores(k + 1)
+            if k in spread:
+                spread_q(on_scalar, 1, spread[k])
             if k >= LAG:
-                scale_and_floor(k - LAG)
+                scale_and_floor(nc.vector, k - LAG)
+        spread_p(on_scalar, 0, 0)
+        spread_p(on_scalar, 0, 1)
 
-        for i in range(SLOT_TILES):
-            regroup_p(nc.scalar.copy, 0, i)
-        assert LAG == 2
-        reciprocal(TOKEN_TILES - 2)
+        reciprocal(6)
         quantise_q_along_tokens(1, 0)
-        scale_and_floor(TOKEN_TILES - 2)
-        reciprocal(TOKEN_TILES - 1)
+        scale_and_floor(nc.vector, 6)
+        reciprocal(7)
         quantise_p(0, 0)
-        scale_and_floor(TOKEN_TILES - 1)
-        for i in range(SLOT_TILES):
-            if i + 1 < SLOT_TILES:
-                quantise_p(0, i + 1)
-            regroup_p(nc.vector.tensor_copy, 1, i)
-            if i >= 1:
-                quantise_p(1, i - 1)
-        quantise_p(1, SLOT_TILES - 1)
-
-        for x in range(QUARTERS):
-            regroup_q([nc.scalar.copy, nc.vector.tensor_copy][x // 2], 1, quarter(1, x))
+        scale_and_floor(nc.vector, 7)
+        quantise_p(0, 1)
+        regroup_p(on_vector, 1, 0)
+        quantise_p(0, 2)
+        quantise_p(1, 0)
+        regroup_p(on_vector, 1, 1)
+        quantise_p(0, 3)
+        quantise_p(1, 1)
+        regroup_p(on_vector, 1, 2)
+        regroup_p(on_vector, 1, 3)
+        quantise_p(1, 2)
+        quantise_p(1, 3)
         quantise_q_along_tokens(1, 1)
-
         first_pass(0, 0)
+        first_pass(1, 0)
+        first_pass(2, 0)
+        first_pass(0, 1)
         for i in range(SLOT_TILES):
-            if i + 1 < SLOT_TILES:
-                first_pass(i + 1, 0)
-            last_pass_and_store(i, 0, nc.scalar.copy)
+            last_pass_and_store(i, 0, on_scalar)
+            if i == 0:
+                first_pass(3, 0)
+            else:
+                first_pass(i, 1)
         for i in range(SLOT_TILES):
-            first_pass(i, 1)
-        for i in range(SLOT_TILES):
-            last_pass_and_store(i, 1, [nc.scalar.copy, nc.vector.tensor_copy][i % 2])
+            last_pass_and_store(i, 1, [on_vector, on_scalar][i % 2])

@@ -69,9 +69,6 @@ def tile_memorymodule_pa_kernel(tc, q, mem, out):
         identity = keep.tile([P, P], F32)
         masks.make_identity(nc, identity[:])
 
-        identity_bf16 = keep.tile([P, P], BF16)
-        masks.make_identity(nc, identity_bf16[:])
-
         zero = keep.tile([P, 1], F32)
         one = keep.tile([P, 1], F32)
         nc.vector.memset(zero[:], 0.0)
@@ -163,21 +160,6 @@ def tile_memorymodule_pa_kernel(tc, q, mem, out):
         def regroup_q(copy, g, columns):
             regroup(copy, qt_grouped[:, g, columns, :], q_columns(g, columns))
 
-        def spread_q(copy, g, x):
-            columns = slice(x * 256, (x + 1) * 256)
-            spread = banks.tile([P, 256, PACK], BF16, tag="bank")
-            rows = q_columns(g, columns)
-            for y in range(2):
-                part = slice(y * 128, (y + 1) * 128)
-                nc.tensor.matmul(
-                    out=spread[:, part, :],
-                    lhsT=identity_bf16[:],
-                    rhs=rows[:, :, part].rearrange("p j c -> p c j"),
-                    start=True,
-                    stop=True,
-                )
-            copy(out=qt_grouped[:, g, columns, :], in_=spread[:])
-
         def quantise_q_along_tokens(g, n):
             nc.vector.quantize_mx(
                 out=qt_codes[:, g, half(n)].bitcast(FP8X4),
@@ -234,21 +216,6 @@ def tile_memorymodule_pa_kernel(tc, q, mem, out):
         def regroup_p(copy, g, i):
             slots = slice(i * P, (i + 1) * P)
             regroup(copy, p_grouped[:, g, slots, :], p_rows[:, g, :, slots])
-
-        def spread_p(copy, g, x):
-            slots = slice(x * 256, (x + 1) * 256)
-            spread = banks.tile([P, 256, PACK], BF16, tag="bank")
-            for y in range(2):
-                part = slice(y * 128, (y + 1) * 128)
-                rows = p_rows[:, g, :, slots][:, :, part]
-                nc.tensor.matmul(
-                    out=spread[:, part, :],
-                    lhsT=identity_bf16[:],
-                    rhs=rows.rearrange("p j s -> p s j"),
-                    start=True,
-                    stop=True,
-                )
-            copy(out=p_grouped[:, g, slots, :], in_=spread[:])
 
         def quantise_p(g, i):
             slots = slice(i * P, (i + 1) * P)
@@ -312,7 +279,6 @@ def tile_memorymodule_pa_kernel(tc, q, mem, out):
         regroup_q(on_vector, 1, piece(0, 1, 4))
         quantise_q_along_width(4, 1)
 
-        spread = {0: 1, 2: 2, 4: 3}
         for k in range(TOKEN_TILES):
             if k >= LAG:
                 reciprocal(k - LAG)
@@ -323,12 +289,14 @@ def tile_memorymodule_pa_kernel(tc, q, mem, out):
             exponential(k)
             if k + 1 < TOKEN_TILES:
                 multiply_scores(k + 1)
-            if k in spread:
-                spread_q(on_scalar, 1, spread[k])
+            if k < 4:
+                regroup_q(on_scalar, 1, piece(0, 4 + k, 8))
+            elif k >= 6:
+                regroup_p(on_scalar, 0, k - 6)
             if k >= LAG:
                 scale_and_floor(nc.vector, k - LAG)
-        spread_p(on_scalar, 0, 0)
-        spread_p(on_scalar, 0, 1)
+        regroup_p(on_scalar, 0, 2)
+        regroup_p(on_scalar, 0, 3)
 
         reciprocal(6)
         quantise_q_along_tokens(1, 0)
@@ -338,25 +306,30 @@ def tile_memorymodule_pa_kernel(tc, q, mem, out):
         scale_and_floor(nc.vector, 7)
         quantise_p(0, 1)
         regroup_p(on_vector, 1, 0)
-        quantise_p(0, 2)
-        quantise_p(1, 0)
         regroup_p(on_vector, 1, 1)
-        quantise_p(0, 3)
+        quantise_p(1, 0)
+        quantise_p(0, 2)
         quantise_p(1, 1)
         regroup_p(on_vector, 1, 2)
+        quantise_p(0, 3)
         regroup_p(on_vector, 1, 3)
         quantise_p(1, 2)
+        regroup_q(on_vector, 1, piece(1, 0, 4))
         quantise_p(1, 3)
+        for x in range(1, 4):
+            regroup_q(on_vector, 1, piece(1, x, 4))
         quantise_q_along_tokens(1, 1)
         first_pass(0, 0)
         first_pass(1, 0)
-        first_pass(2, 0)
         first_pass(0, 1)
-        for i in range(SLOT_TILES):
-            last_pass_and_store(i, 0, on_scalar)
-            if i == 0:
-                first_pass(3, 0)
-            else:
-                first_pass(i, 1)
+        last_pass_and_store(0, 0, on_scalar)
+        first_pass(2, 0)
+        last_pass_and_store(1, 0, on_scalar)
+        first_pass(3, 0)
+        last_pass_and_store(2, 0, on_scalar)
+        first_pass(1, 1)
+        last_pass_and_store(3, 0, on_scalar)
+        first_pass(2, 1)
+        first_pass(3, 1)
         for i in range(SLOT_TILES):
             last_pass_and_store(i, 1, [on_vector, on_scalar][i % 2])

@@ -199,8 +199,8 @@ def tile_memorymodule_pa_kernel(tc, q, mem, out):
                 accum_out=totals[:, k : k + 1],
             )
 
-        def reciprocal(k):
-            nc.vector.reciprocal(out=inverse[:, k : k + 1], in_=totals[:, k : k + 1])
+        def reciprocals(k):
+            nc.vector.reciprocal(out=inverse[:, k : k + 2], in_=totals[:, k : k + 2])
 
         def scale_and_floor(engine, k):
             g, j = divmod(k, PACK)
@@ -276,48 +276,70 @@ def tile_memorymodule_pa_kernel(tc, q, mem, out):
         flip_two_tiles(6, 0, on_scalar)
         flip_two_tiles(6, 1, on_scalar)
         quantise_q_along_width(4, 0)
-        regroup_q(on_vector, 1, piece(0, 1, 4))
+        maximum(0)
         quantise_q_along_width(4, 1)
-
-        for k in range(TOKEN_TILES):
-            if k >= LAG:
-                reciprocal(k - LAG)
-            maximum(k)
-            if k == 0:
-                quantise_q_along_width(6, 0)
-                quantise_q_along_width(6, 1)
-            exponential(k)
-            if k + 1 < TOKEN_TILES:
-                multiply_scores(k + 1)
-            if k < 4:
-                regroup_q(on_scalar, 1, piece(0, 4 + k, 8))
-            elif k >= 6:
-                regroup_p(on_scalar, 0, k - 6)
-            if k >= LAG:
-                scale_and_floor(nc.vector, k - LAG)
+        regroup_q(on_vector, 1, piece(0, 1, 4))
+        multiply_scores(1)
+        quantise_q_along_width(6, 0)
+        maximum(1)
+        quantise_q_along_width(6, 1)
+        exponential(0)
+        multiply_scores(2)
+        regroup_q(on_scalar, 1, piece(0, 4, 8))
+        multiply_scores(3)
+        maximum(2)
+        exponential(1)
+        regroup_q(on_scalar, 1, piece(0, 5, 8))
+        multiply_scores(4)
+        reciprocals(0)
+        maximum(3)
+        exponential(2)
+        scale_and_floor(nc.vector, 0)
+        regroup_q(on_scalar, 1, piece(0, 6, 8))
+        multiply_scores(5)
+        maximum(4)
+        exponential(3)
+        scale_and_floor(nc.vector, 1)
+        regroup_q(on_scalar, 1, piece(0, 7, 8))
+        multiply_scores(6)
+        reciprocals(2)
+        maximum(5)
+        exponential(4)
+        scale_and_floor(nc.vector, 2)
+        multiply_scores(7)
+        maximum(6)
+        exponential(5)
+        scale_and_floor(nc.vector, 3)
+        reciprocals(4)
+        maximum(7)
+        exponential(6)
+        regroup_p(on_scalar, 0, 0)
+        scale_and_floor(nc.vector, 4)
+        quantise_q_along_tokens(1, 0)
+        scale_and_floor(nc.vector, 5)
+        exponential(7)
+        regroup_p(on_scalar, 0, 1)
         regroup_p(on_scalar, 0, 2)
         regroup_p(on_scalar, 0, 3)
-
-        reciprocal(6)
-        quantise_q_along_tokens(1, 0)
-        scale_and_floor(nc.vector, 6)
-        reciprocal(7)
+        regroup_q(on_scalar, 1, piece(1, 0, 4))
+        reciprocals(6)
         quantise_p(0, 0)
+        scale_and_floor(nc.vector, 6)
         scale_and_floor(nc.vector, 7)
         quantise_p(0, 1)
         regroup_p(on_vector, 1, 0)
-        regroup_p(on_vector, 1, 1)
-        quantise_p(1, 0)
         quantise_p(0, 2)
+        quantise_p(1, 0)
+        regroup_p(on_vector, 1, 1)
+        quantise_p(0, 3)
         quantise_p(1, 1)
         regroup_p(on_vector, 1, 2)
-        quantise_p(0, 3)
-        regroup_p(on_vector, 1, 3)
+        regroup_q(on_vector, 1, piece(1, 1, 4))
         quantise_p(1, 2)
-        regroup_q(on_vector, 1, piece(1, 0, 4))
+        regroup_p(on_vector, 1, 3)
+        regroup_q(on_vector, 1, piece(1, 2, 4))
         quantise_p(1, 3)
-        for x in range(1, 4):
-            regroup_q(on_vector, 1, piece(1, x, 4))
+        regroup_q(on_vector, 1, piece(1, 3, 4))
         quantise_q_along_tokens(1, 1)
         first_pass(0, 0)
         first_pass(1, 0)

@@ -69,10 +69,13 @@ def tile_memorymodule_pa_kernel(tc, q, mem, out):
         identity = keep.tile([P, P], F32)
         masks.make_identity(nc, identity[:])
 
+        zeros = keep.tile([P, P], BF16)
+        nc.gpsimd.memset(zeros[:], 0.0)
         zero = keep.tile([P, 1], F32)
         one = keep.tile([P, 1], F32)
         nc.vector.memset(zero[:], 0.0)
         nc.scalar.activation(out=one[:], in_=zero[:], func=ACT.Exp)
+        gate = keep.tile([P, 1], F32)
 
         q_halves = [keep.tile([P, PACK, N_BANK], BF16, name="q_half%d" % h) for h in range(WIDTH_HALVES)]
         q_last = keep.tile([P, PACK, WIDTH], BF16)
@@ -157,14 +160,20 @@ def tile_memorymodule_pa_kernel(tc, q, mem, out):
                 in_=qw_grouped[:, first * PACK : (first + 2 * P) * PACK],
             )
 
+        def on_gpsimd(out, in_):
+            nc.gpsimd.tensor_scalar(out=out, in0=in_, scalar1=gate[:], scalar2=0.0, op0=ALU.mult, op1=ALU.add)
+
+        def floor_on_vector(out, in_):
+            nc.vector.tensor_scalar(out=out, in0=in_, scalar1=FLOOR, scalar2=None, op0=ALU.max)
+
         def regroup_q(copy, g, columns):
             regroup(copy, qt_grouped[:, g, columns, :], q_columns(g, columns))
 
-        def quantise_q_along_tokens(g, n):
+        def quantise_q_along_tokens(g, columns):
             nc.vector.quantize_mx(
-                out=qt_codes[:, g, half(n)].bitcast(FP8X4),
-                scales=qt_scales[:, g, half(n)],
-                in_=qt_grouped[:, g, half(n), :].rearrange("p c j -> p (c j)"),
+                out=qt_codes[:, g, columns].bitcast(FP8X4),
+                scales=qt_scales[:, g, columns],
+                in_=qt_grouped[:, g, columns, :].rearrange("p c j -> p (c j)"),
             )
 
         score_banks = {}
@@ -202,6 +211,23 @@ def tile_memorymodule_pa_kernel(tc, q, mem, out):
         def reciprocals(k):
             nc.vector.reciprocal(out=inverse[:, k : k + 2], in_=totals[:, k : k + 2])
 
+        def scale(k):
+            g, j = divmod(k, PACK)
+            nc.gpsimd.tensor_scalar(
+                out=p_rows[:, g, j, :],
+                in0=exp_rows[:, k, :],
+                scalar1=inverse[:, k : k + 1],
+                scalar2=0.0,
+                op0=ALU.mult,
+                op1=ALU.add,
+            )
+
+        def reciprocal(k):
+            nc.vector.reciprocal(out=inverse[:, k : k + 1], in_=totals[:, k : k + 1])
+
+        def reciprocals_of(first, count):
+            nc.vector.reciprocal(out=inverse[:, first : first + count], in_=totals[:, first : first + count])
+
         def scale_and_floor(engine, k):
             g, j = divmod(k, PACK)
             engine.tensor_scalar(
@@ -227,26 +253,31 @@ def tile_memorymodule_pa_kernel(tc, q, mem, out):
 
         sums = {}
 
-        def matmul_2_pass(i, n, g):
+        def matmul_2_pass(i, columns, g):
             slots = slice(i * P, (i + 1) * P)
             nc.tensor.matmul_mx(
-                out=sums[(i, n)][:],
+                out=sums[(i, columns.start)][:, : columns.stop - columns.start],
                 lhsT=p_codes[:, g, slots].bitcast(FP8X4),
                 lhsT_scale=p_scales[:, g, slots],
-                rhs=qt_codes[:, g, half(n)].bitcast(FP8X4),
-                rhs_scale=qt_scales[:, g, half(n)],
+                rhs=qt_codes[:, g, columns].bitcast(FP8X4),
+                rhs_scale=qt_scales[:, g, columns],
                 start=(g == 0),
                 stop=(g == TOKEN_PASSES - 1),
             )
 
-        def first_pass(i, n):
-            sums[(i, n)] = banks.tile([P, N_BANK], F32, tag="bank", name="sums%d%d" % (i, n))
-            matmul_2_pass(i, n, 0)
+        def first_pass(i, columns):
+            sums[(i, columns.start)] = banks.tile([P, N_BANK], F32, tag="bank", name="sums%d_%d" % (i, columns.start))
+            matmul_2_pass(i, columns, 0)
 
-        def last_pass_and_store(i, n, copy):
-            matmul_2_pass(i, n, 1)
-            copy(out=results[:, i, half(n)], in_=sums[(i, n)][:])
-            nc.sync.dma_start(out=out_tiles[i][:, half(n)], in_=results[:, i, half(n)])
+        def last_pass_and_store(i, columns, copy):
+            matmul_2_pass(i, columns, 1)
+            copy(out=results[:, i, columns], in_=sums[(i, columns.start)][:, : columns.stop - columns.start])
+            nc.sync.dma_start(out=out_tiles[i][:, columns], in_=results[:, i, columns])
+
+        def keep_clock(several_rows):
+            unread = banks.tile([P, N_BANK], F32, tag="bank")
+            for rows in several_rows:
+                nc.tensor.matmul(out=unread[:], lhsT=zeros[:], rhs=rows, start=True, stop=True)
 
         on_scalar, on_vector = nc.scalar.copy, nc.vector.tensor_copy
         flip_two_tiles(0, 0, on_scalar)
@@ -257,7 +288,7 @@ def tile_memorymodule_pa_kernel(tc, q, mem, out):
         flip_two_tiles(0, 1, on_scalar)
         flip_two_tiles(2, 1, on_scalar)
         quantise_q_along_width(2, 0)
-        quantise_q_along_tokens(0, 0)
+        quantise_q_along_tokens(0, half(0))
         quantise_q_along_width(0, 1)
         regroup_q(on_scalar, 0, piece(1, 3, 4))
         regroup_q(on_vector, 0, piece(1, 0, 2))
@@ -266,92 +297,86 @@ def tile_memorymodule_pa_kernel(tc, q, mem, out):
         for i in (0, 2):
             for h in range(WIDTH_PASSES):
                 flip_two_mem_tiles(i, h, on_scalar)
-        quantise_q_along_tokens(0, 1)
+        quantise_q_along_tokens(0, half(1))
         flip_two_tiles(4, 0, on_scalar)
         flip_two_tiles(4, 1, on_scalar)
         quantise_mem(0)
         quantise_mem(1)
-        multiply_scores(0)
-        regroup_q(on_scalar, 1, piece(0, 0, 4))
+        quantise_q_along_width(4, 0)
+        regroup_q(on_vector, 1, piece(0, 0, 4))
         flip_two_tiles(6, 0, on_scalar)
         flip_two_tiles(6, 1, on_scalar)
-        quantise_q_along_width(4, 0)
-        maximum(0)
+        regroup_q(on_scalar, 1, piece(0, 2, 4))
+        multiply_scores(0)
         quantise_q_along_width(4, 1)
-        regroup_q(on_vector, 1, piece(0, 1, 4))
         multiply_scores(1)
+        regroup_q(on_vector, 1, piece(0, 1, 4))
         quantise_q_along_width(6, 0)
-        maximum(1)
+        regroup_q(on_vector, 1, piece(0, 3, 4))
         quantise_q_along_width(6, 1)
+        nc.vector.memset(gate[:], 1.0)
+        for x in range(4):
+            regroup_q(on_gpsimd, 1, piece(1, x, 4))
+        for k in range(2, TOKEN_TILES):
+            multiply_scores(k)
+        maximum(0)
         exponential(0)
-        multiply_scores(2)
-        regroup_q(on_scalar, 1, piece(0, 4, 8))
-        multiply_scores(3)
-        maximum(2)
+        maximum(1)
         exponential(1)
-        regroup_q(on_scalar, 1, piece(0, 5, 8))
-        multiply_scores(4)
-        reciprocals(0)
-        maximum(3)
+        maximum(2)
         exponential(2)
-        scale_and_floor(nc.vector, 0)
-        regroup_q(on_scalar, 1, piece(0, 6, 8))
-        multiply_scores(5)
-        maximum(4)
+        maximum(3)
         exponential(3)
-        scale_and_floor(nc.vector, 1)
-        regroup_q(on_scalar, 1, piece(0, 7, 8))
-        multiply_scores(6)
-        reciprocals(2)
-        maximum(5)
+        maximum(4)
         exponential(4)
-        scale_and_floor(nc.vector, 2)
-        multiply_scores(7)
-        maximum(6)
+        maximum(5)
+        reciprocals_of(0, 4)
         exponential(5)
-        scale_and_floor(nc.vector, 3)
-        reciprocals(4)
-        maximum(7)
+        maximum(6)
+        scale_and_floor(nc.vector, 0)
         exponential(6)
-        regroup_p(on_scalar, 0, 0)
-        scale_and_floor(nc.vector, 4)
-        quantise_q_along_tokens(1, 0)
-        scale_and_floor(nc.vector, 5)
+        maximum(7)
         exponential(7)
+        scale_and_floor(nc.vector, 1)
+        scale_and_floor(nc.vector, 2)
+        reciprocals_of(4, 2)
+        scale_and_floor(nc.vector, 3)
+        quantise_q_along_tokens(1, piece(0, 0, 2))
+        scale_and_floor(nc.vector, 4)
+        reciprocals_of(6, 2)
+        scale_and_floor(nc.vector, 5)
+        regroup_p(on_scalar, 0, 0)
         regroup_p(on_scalar, 0, 1)
         regroup_p(on_scalar, 0, 2)
-        regroup_p(on_scalar, 0, 3)
-        regroup_q(on_scalar, 1, piece(1, 0, 4))
-        reciprocals(6)
-        quantise_p(0, 0)
         scale_and_floor(nc.vector, 6)
         scale_and_floor(nc.vector, 7)
-        quantise_p(0, 1)
+        keep_clock([p_rows[:, k // PACK, k % PACK, :] for k in (0, 2, 3, 4, 6)])
+        quantise_p(0, 0)
         regroup_p(on_vector, 1, 0)
-        quantise_p(0, 2)
+        quantise_p(0, 1)
         quantise_p(1, 0)
-        regroup_p(on_vector, 1, 1)
-        quantise_p(0, 3)
+        regroup_p(on_scalar, 1, 1)
+        quantise_q_along_tokens(1, piece(0, 1, 2))
         quantise_p(1, 1)
         regroup_p(on_vector, 1, 2)
-        regroup_q(on_vector, 1, piece(1, 1, 4))
+        quantise_q_along_tokens(1, half(1))
+        quantise_p(0, 2)
         quantise_p(1, 2)
         regroup_p(on_vector, 1, 3)
-        regroup_q(on_vector, 1, piece(1, 2, 4))
+        regroup_p(on_vector, 0, 3)
         quantise_p(1, 3)
-        regroup_q(on_vector, 1, piece(1, 3, 4))
-        quantise_q_along_tokens(1, 1)
-        first_pass(0, 0)
-        first_pass(1, 0)
-        first_pass(0, 1)
-        last_pass_and_store(0, 0, on_scalar)
-        first_pass(2, 0)
-        last_pass_and_store(1, 0, on_scalar)
-        first_pass(3, 0)
-        last_pass_and_store(2, 0, on_scalar)
-        first_pass(1, 1)
-        last_pass_and_store(3, 0, on_scalar)
-        first_pass(2, 1)
-        first_pass(3, 1)
-        for i in range(SLOT_TILES):
-            last_pass_and_store(i, 1, [on_vector, on_scalar][i % 2])
+        quantise_p(0, 3)
+        first_pass(0, piece(0, 0, 2))
+        first_pass(0, piece(0, 1, 2))
+        first_pass(0, half(1))
+        last_pass_and_store(0, piece(0, 0, 2), on_scalar)
+        last_pass_and_store(0, piece(0, 1, 2), on_scalar)
+        first_pass(1, half(0))
+        last_pass_and_store(1, half(0), on_scalar)
+        first_pass(1, half(1))
+        for i in range(2):
+            last_pass_and_store(i, half(1), on_scalar)
+        for i in range(2, SLOT_TILES):
+            for n in range(WIDTH_HALVES):
+                first_pass(i, half(n))
+                last_pass_and_store(i, half(n), [on_vector, on_scalar][(i + n) % 2])

@@ -225,6 +225,12 @@ def tile_memorymodule_pa_kernel(tc, q, mem, out):
         def reciprocal(k):
             nc.vector.reciprocal(out=inverse[:, k : k + 1], in_=totals[:, k : k + 1])
 
+        def scale_on_scalar(k):
+            g, j = divmod(k, PACK)
+            nc.scalar.activation(
+                out=p_rows[:, g, j, :], in_=exp_rows[:, k, :], func=ACT.Copy, scale=inverse[:, k : k + 1]
+            )
+
         def reciprocals_of(first, count):
             nc.vector.reciprocal(out=inverse[:, first : first + count], in_=totals[:, first : first + count])
 
@@ -307,65 +313,67 @@ def tile_memorymodule_pa_kernel(tc, q, mem, out):
         flip_two_tiles(6, 0, on_scalar)
         flip_two_tiles(6, 1, on_scalar)
         regroup_q(on_scalar, 1, piece(0, 2, 4))
-        multiply_scores(0)
+        regroup_q(on_scalar, 1, piece(1, 0, 4))
         quantise_q_along_width(4, 1)
-        multiply_scores(1)
+        multiply_scores(4)
+        multiply_scores(5)
         regroup_q(on_vector, 1, piece(0, 1, 4))
         quantise_q_along_width(6, 0)
         regroup_q(on_vector, 1, piece(0, 3, 4))
         quantise_q_along_width(6, 1)
         nc.vector.memset(gate[:], 1.0)
-        for x in range(4):
+        for x in range(1, 4):
             regroup_q(on_gpsimd, 1, piece(1, x, 4))
-        for k in range(2, TOKEN_TILES):
+        for k in (0, 1, 2, 3, 6, 7):
             multiply_scores(k)
+        maximum(4)
+        exponential(4)
+        maximum(5)
+        exponential(5)
         maximum(0)
         exponential(0)
         maximum(1)
+        reciprocals_of(4, 2)
+        scale(4)
+        scale(5)
         exponential(1)
         maximum(2)
         exponential(2)
         maximum(3)
         exponential(3)
-        maximum(4)
-        exponential(4)
-        maximum(5)
-        reciprocals_of(0, 4)
-        exponential(5)
+        reciprocals_of(0, 2)
         maximum(6)
         scale_and_floor(nc.vector, 0)
         exponential(6)
         maximum(7)
         exponential(7)
+        reciprocals_of(2, 2)
         scale_and_floor(nc.vector, 1)
         scale_and_floor(nc.vector, 2)
-        reciprocals_of(4, 2)
         scale_and_floor(nc.vector, 3)
         quantise_q_along_tokens(1, piece(0, 0, 2))
-        scale_and_floor(nc.vector, 4)
         reciprocals_of(6, 2)
-        scale_and_floor(nc.vector, 5)
+        quantise_q_along_tokens(1, piece(0, 1, 2))
         regroup_p(on_scalar, 0, 0)
         regroup_p(on_scalar, 0, 1)
         regroup_p(on_scalar, 0, 2)
         scale_and_floor(nc.vector, 6)
         scale_and_floor(nc.vector, 7)
-        keep_clock([p_rows[:, k // PACK, k % PACK, :] for k in (0, 2, 3, 4, 6)])
+        keep_clock([p_rows[:, k // PACK, k % PACK, :] for k in (0, 1, 2, 3, 6)])
         quantise_p(0, 0)
-        regroup_p(on_vector, 1, 0)
+        regroup_p(floor_on_vector, 1, 0)
         quantise_p(0, 1)
         quantise_p(1, 0)
-        regroup_p(on_scalar, 1, 1)
-        quantise_q_along_tokens(1, piece(0, 1, 2))
-        quantise_p(1, 1)
-        regroup_p(on_vector, 1, 2)
-        quantise_q_along_tokens(1, half(1))
+        regroup_p(floor_on_vector, 1, 1)
+        regroup_p(on_scalar, 0, 3)
         quantise_p(0, 2)
+        quantise_p(1, 1)
+        quantise_q_along_tokens(1, half(1))
+        regroup_p(floor_on_vector, 1, 2)
+        regroup_p(floor_on_vector, 1, 3)
         quantise_p(1, 2)
-        regroup_p(on_vector, 1, 3)
-        regroup_p(on_vector, 0, 3)
-        quantise_p(1, 3)
         quantise_p(0, 3)
+        quantise_p(1, 3)
         first_pass(0, piece(0, 0, 2))
         first_pass(0, piece(0, 1, 2))
         first_pass(0, half(1))

@@ -343,48 +343,52 @@ def tile_memorymodule_pa_kernel(tc, q, mem, out):
         exponential(3)
         reciprocals_of(0, 2)
         maximum(6)
-        scale_and_floor(nc.vector, 0)
         exponential(6)
         maximum(7)
         exponential(7)
+        scale_and_floor(nc.vector, 0)
         reciprocals_of(2, 2)
         scale_and_floor(nc.vector, 1)
+        reciprocals_of(6, 1)
+        scale_on_scalar(6)
         scale_and_floor(nc.vector, 2)
         scale_and_floor(nc.vector, 3)
         quantise_q_along_tokens(1, piece(0, 0, 2))
-        reciprocals_of(6, 2)
+        reciprocals_of(7, 1)
         quantise_q_along_tokens(1, piece(0, 1, 2))
         regroup_p(on_scalar, 0, 0)
         regroup_p(on_scalar, 0, 1)
         regroup_p(on_scalar, 0, 2)
-        scale_and_floor(nc.vector, 6)
         scale_and_floor(nc.vector, 7)
         keep_clock([p_rows[:, k // PACK, k % PACK, :] for k in (0, 1, 2, 3, 6)])
         quantise_p(0, 0)
         regroup_p(floor_on_vector, 1, 0)
         quantise_p(0, 1)
         quantise_p(1, 0)
+        quantise_q_along_tokens(1, piece(1, 0, 2))
         regroup_p(floor_on_vector, 1, 1)
-        regroup_p(on_scalar, 0, 3)
-        quantise_p(0, 2)
+        quantise_q_along_tokens(1, piece(1, 1, 2))
         quantise_p(1, 1)
-        quantise_q_along_tokens(1, half(1))
+        quantise_p(0, 2)
         regroup_p(floor_on_vector, 1, 2)
+        regroup_p(on_vector, 0, 3)
         regroup_p(floor_on_vector, 1, 3)
         quantise_p(1, 2)
         quantise_p(0, 3)
         quantise_p(1, 3)
-        first_pass(0, piece(0, 0, 2))
-        first_pass(0, piece(0, 1, 2))
-        first_pass(0, half(1))
-        last_pass_and_store(0, piece(0, 0, 2), on_scalar)
-        last_pass_and_store(0, piece(0, 1, 2), on_scalar)
+        for x in range(2):
+            first_pass(0, piece(0, x, 2))
+        for x in range(2):
+            first_pass(0, piece(1, x, 2))
+        for x in range(2):
+            last_pass_and_store(0, piece(0, x, 2), on_scalar)
+        last_pass_and_store(0, piece(1, 0, 2), on_scalar)
         first_pass(1, half(0))
+        last_pass_and_store(0, piece(1, 1, 2), on_scalar)
         last_pass_and_store(1, half(0), on_scalar)
         first_pass(1, half(1))
-        for i in range(2):
-            last_pass_and_store(i, half(1), on_scalar)
+        last_pass_and_store(1, half(1), on_scalar)
         for i in range(2, SLOT_TILES):
             for n in range(WIDTH_HALVES):
                 first_pass(i, half(n))
-                last_pass_and_store(i, half(n), [on_vector, on_scalar][(i + n) % 2])
+                last_pass_and_store(i, half(n), [on_scalar, on_vector][n])

from contextlib import ExitStack

import concourse.masks as masks
import concourse.mybir as mybir

F32 = mybir.dt.float32
BF16 = mybir.dt.bfloat16
U32 = mybir.dt.uint32
U8 = mybir.dt.uint8
FP8X4 = mybir.dt.float8_e4m3fn_x4
ACT = mybir.ActivationFunctionType
ALU = mybir.AluOpType
AXIS = mybir.AxisListType

P = 128
PACK = 4
K_PASS = P * PACK
N_BANK = 512

TOKENS = 1024
WIDTH = 1024
SLOTS = 512
FLOOR = 1e-8

TOKEN_PASSES = TOKENS // K_PASS
WIDTH_PASSES = WIDTH // K_PASS
TOKEN_TILES = TOKENS // P
SLOT_TILES = SLOTS // P
WIDTH_HALVES = WIDTH // N_BANK
PAIR = 2
WORDS = WIDTH // PAIR
RUN = 4
LAG = 2

FLOPS = 2 * 2 * TOKENS * WIDTH * SLOTS


def half(n):
    return slice(n * N_BANK, (n + 1) * N_BANK)


def piece(n, x, parts):
    width = N_BANK // parts
    return slice(n * N_BANK + x * width, n * N_BANK + (x + 1) * width)


def flip_rows(nc, banks, identity, blocks, grouped_words, copy):
    flipped = banks.tile([P, 2, PAIR, P], F32, tag="bank")
    for b in range(2):
        for u in range(PAIR):
            nc.tensor.transpose(flipped[:, b, u, :], blocks[b][u], identity[:])
    copy(out=grouped_words, in_=flipped[:].rearrange("p b u r -> p b r u"))


def regroup(copy, grouped, rows):
    copy(
        out=grouped.rearrange("p (c i) j -> p c j i", i=RUN),
        in_=rows.rearrange("p j (c i) -> p c j i", i=RUN),
    )


def tile_memorymodule_pa_kernel(tc, q, mem, out):
    nc = tc.nc
    with ExitStack() as ctx:
        keep = ctx.enter_context(tc.tile_pool(name="keep", bufs=1))
        banks = ctx.enter_context(tc.psum_pool(name="banks", bufs=8))
        ctx.enter_context(tc.manual_schedule())

        identity = keep.tile([P, P], F32)
        masks.make_identity(nc, identity[:])

        zeros = keep.tile([P, P], BF16)
        nc.gpsimd.memset(zeros[:], 0.0)
        zero = keep.tile([P, 1], F32)
        one = keep.tile([P, 1], F32)
        nc.vector.memset(zero[:], 0.0)
        nc.scalar.activation(out=one[:], in_=zero[:], func=ACT.Exp)
        gate = keep.tile([P, 1], F32)

        q_halves = [keep.tile([P, PACK, N_BANK], BF16, name="q_half%d" % h) for h in range(WIDTH_HALVES)]
        q_last = keep.tile([P, PACK, WIDTH], BF16)
        mem_rows = keep.tile([P, SLOT_TILES * WIDTH], BF16)
        mem_grouped = keep.tile([P, WIDTH_PASSES * SLOTS * PACK], BF16, align_bytes=64)
        mem_codes = keep.tile([P, WIDTH_PASSES, SLOTS], U32, align_bytes=64)
        mem_scales = keep.tile([P, WIDTH_PASSES, SLOTS], U8, align_bytes=64)
        qw_grouped = keep.tile([P, WIDTH_PASSES * TOKENS * PACK], BF16, align_bytes=64)
        qw_codes = keep.tile([P, WIDTH_PASSES, TOKENS], U32, align_bytes=64)
        qw_scales = keep.tile([P, WIDTH_PASSES, TOKENS], U8, align_bytes=64)
        qt_grouped = keep.tile([P, TOKEN_PASSES, WIDTH, PACK], BF16, align_bytes=64)
        qt_codes = keep.tile([P, TOKEN_PASSES, WIDTH], U32, align_bytes=64)
        qt_scales = keep.tile([P, TOKEN_PASSES, WIDTH], U8, align_bytes=64)
        neg_max = keep.tile([P, TOKEN_TILES], F32)
        totals = keep.tile([P, TOKEN_TILES], F32)
        inverse = keep.tile([P, TOKEN_TILES], F32)
        exp_rows = keep.tile([P, TOKEN_TILES, SLOTS], F32)
        p_rows = keep.tile([P, TOKEN_PASSES, PACK, SLOTS], BF16)
        p_grouped = keep.tile([P, TOKEN_PASSES, SLOTS, PACK], BF16, align_bytes=64)
        p_codes = keep.tile([P, TOKEN_PASSES, SLOTS], U32, align_bytes=64)
        p_scales = keep.tile([P, TOKEN_PASSES, SLOTS], U8, align_bytes=64)
        results = keep.tile([P, SLOT_TILES, WIDTH], F32)

        q_view = q.rearrange("(g p j) c -> g p j c", g=TOKEN_PASSES, j=PACK)
        mem_view = mem.rearrange("(p i) c -> p i c", i=SLOT_TILES)
        out_tiles = out.rearrange("(p i) c -> i p c", i=SLOT_TILES)
        mem_rows_view = mem_rows[:].rearrange("p (i c) -> p i c", i=SLOT_TILES)

        for h in range(WIDTH_PASSES):
            for first in range(0, PACK, 2):
                pair = slice(first, first + 2)
                nc.sync.dma_start(out=q_halves[h][:, pair, :], in_=q_view[0][:, pair, half(h)])
        for first in range(0, SLOT_TILES, 2):
            pair = slice(first, first + 2)
            nc.sync.dma_start(out=mem_rows_view[:, pair, :], in_=mem_view[:, pair, :])
        for first in range(0, PACK, 2):
            pair = slice(first, first + 2)
            nc.sync.dma_start(out=q_last[:, pair, :], in_=q_view[1][:, pair, :])

        mem_grouped_words = mem_grouped[:].bitcast(F32).rearrange(
            "p (h s u) -> p h s u", h=WIDTH_PASSES, u=PAIR
        )
        qw_grouped_words = qw_grouped[:].bitcast(F32).rearrange(
            "p (h k r u) -> p h k r u", h=WIDTH_PASSES, k=TOKEN_TILES, u=PAIR
        )

        def words_of(rows):
            words = rows.bitcast(F32)
            return [words[:, u * P : (u + 1) * P] for u in range(PAIR)]

        def q_columns(g, columns):
            if g == 0:
                h, first = divmod(columns.start, N_BANK)
                return q_halves[h][:, :, first : first + columns.stop - columns.start]
            return q_last[:, :, columns]


        def flip_two_mem_tiles(i, h, copy):
            slots = slice(i * P, (i + 2) * P)
            blocks = [words_of(mem_rows_view[:, i + b, half(h)]) for b in range(2)]
            grouped = mem_grouped_words[:, h, slots, :].rearrange("p (b r) u -> p b r u", b=2)
            flip_rows(nc, banks, identity, blocks, grouped, copy)

        def quantise_mem(h):
            nc.vector.quantize_mx(
                out=mem_codes[:, h, :].bitcast(FP8X4),
                scales=mem_scales[:, h, :],
                in_=mem_grouped[:, h * SLOTS * PACK : (h + 1) * SLOTS * PACK],
            )

        def flip_two_tiles(k, h, copy):
            g, j = divmod(k, PACK)
            blocks = [words_of(q_columns(g, half(h))[:, j + b, :]) for b in range(2)]
            flip_rows(nc, banks, identity, blocks, qw_grouped_words[:, h, k : k + 2], copy)

        def quantise_q_along_width(k, h):
            tokens = slice(k * P, (k + 2) * P)
            first = h * TOKENS + k * P
            nc.vector.quantize_mx(
                out=qw_codes[:, h, tokens].bitcast(FP8X4),
                scales=qw_scales[:, h, tokens],
                in_=qw_grouped[:, first * PACK : (first + 2 * P) * PACK],
            )

        def on_gpsimd(out, in_):
            nc.gpsimd.tensor_scalar(out=out, in0=in_, scalar1=gate[:], scalar2=0.0, op0=ALU.mult, op1=ALU.add)

        def floor_on_vector(out, in_):
            nc.vector.tensor_scalar(out=out, in0=in_, scalar1=FLOOR, scalar2=None, op0=ALU.max)

        def regroup_q(copy, g, columns):
            regroup(copy, qt_grouped[:, g, columns, :], q_columns(g, columns))

        def quantise_q_along_tokens(g, columns):
            nc.vector.quantize_mx(
                out=qt_codes[:, g, columns].bitcast(FP8X4),
                scales=qt_scales[:, g, columns],
                in_=qt_grouped[:, g, columns, :].rearrange("p c j -> p (c j)"),
            )

        score_banks = {}

        def multiply_scores(k):
            tokens = slice(k * P, (k + 1) * P)
            scores = banks.tile([P, SLOTS], F32, tag="bank")
            for h in range(WIDTH_PASSES):
                nc.tensor.matmul_mx(
                    out=scores[:],
                    lhsT=qw_codes[:, h, tokens].bitcast(FP8X4),
                    lhsT_scale=qw_scales[:, h, tokens],
                    rhs=mem_codes[:, h, :].bitcast(FP8X4),
                    rhs_scale=mem_scales[:, h, :],
                    start=(h == 0),
                    stop=(h == WIDTH_PASSES - 1),
                )
            score_banks[k] = scores

        def maximum(k):
            nc.vector.tensor_reduce(
                out=neg_max[:, k : k + 1], in_=score_banks[k][:], axis=AXIS.X, op=ALU.max, negate=True
            )

        def exponential(k):
            nc.scalar.activation(
                out=exp_rows[:, k, :],
                in_=score_banks[k][:],
                func=ACT.Exp,
                bias=neg_max[:, k : k + 1],
                scale=1.0,
                accum_out=totals[:, k : k + 1],
            )

        def reciprocals(k):
            nc.vector.reciprocal(out=inverse[:, k : k + 2], in_=totals[:, k : k + 2])

        def scale(k):
            g, j = divmod(k, PACK)
            nc.gpsimd.tensor_scalar(
                out=p_rows[:, g, j, :],
                in0=exp_rows[:, k, :],
                scalar1=inverse[:, k : k + 1],
                scalar2=0.0,
                op0=ALU.mult,
                op1=ALU.add,
            )

        def reciprocal(k):
            nc.vector.reciprocal(out=inverse[:, k : k + 1], in_=totals[:, k : k + 1])

        def scale_on_scalar(k):
            g, j = divmod(k, PACK)
            nc.scalar.activation(
                out=p_rows[:, g, j, :], in_=exp_rows[:, k, :], func=ACT.Copy, scale=inverse[:, k : k + 1]
            )

        def reciprocals_of(first, count):
            nc.vector.reciprocal(out=inverse[:, first : first + count], in_=totals[:, first : first + count])

        def scale_and_floor(engine, k):
            g, j = divmod(k, PACK)
            engine.tensor_scalar(
                out=p_rows[:, g, j, :],
                in0=exp_rows[:, k, :],
                scalar1=inverse[:, k : k + 1],
                scalar2=FLOOR,
                op0=ALU.mult,
                op1=ALU.max,
            )

        def regroup_p(copy, g, i):
            slots = slice(i * P, (i + 1) * P)
            regroup(copy, p_grouped[:, g, slots, :], p_rows[:, g, :, slots])

        def quantise_p(g, i):
            slots = slice(i * P, (i + 1) * P)
            nc.vector.quantize_mx(
                out=p_codes[:, g, slots].bitcast(FP8X4),
                scales=p_scales[:, g, slots],
                in_=p_grouped[:, g, slots, :].rearrange("p s j -> p (s j)"),
            )

        sums = {}

        def matmul_2_pass(i, columns, g):
            slots = slice(i * P, (i + 1) * P)
            nc.tensor.matmul_mx(
                out=sums[(i, columns.start)][:, : columns.stop - columns.start],
                lhsT=p_codes[:, g, slots].bitcast(FP8X4),
                lhsT_scale=p_scales[:, g, slots],
                rhs=qt_codes[:, g, columns].bitcast(FP8X4),
                rhs_scale=qt_scales[:, g, columns],
                start=(g == 0),
                stop=(g == TOKEN_PASSES - 1),
            )

        def first_pass(i, columns):
            sums[(i, columns.start)] = banks.tile([P, N_BANK], F32, tag="bank", name="sums%d_%d" % (i, columns.start))
            matmul_2_pass(i, columns, 0)

        def last_pass_and_store(i, columns, copy):
            matmul_2_pass(i, columns, 1)
            copy(out=results[:, i, columns], in_=sums[(i, columns.start)][:, : columns.stop - columns.start])
            nc.sync.dma_start(out=out_tiles[i][:, columns], in_=results[:, i, columns])

        def keep_clock(several_rows):
            unread = banks.tile([P, N_BANK], F32, tag="bank")
            for rows in several_rows:
                nc.tensor.matmul(out=unread[:], lhsT=zeros[:], rhs=rows, start=True, stop=True)

        on_scalar, on_vector = nc.scalar.copy, nc.vector.tensor_copy
        flip_two_tiles(0, 0, on_scalar)
        flip_two_tiles(2, 0, on_scalar)
        regroup_q(on_vector, 0, piece(0, 0, 2))
        quantise_q_along_width(0, 0)
        regroup_q(on_vector, 0, piece(0, 1, 2))
        flip_two_tiles(0, 1, on_scalar)
        flip_two_tiles(2, 1, on_scalar)
        quantise_q_along_width(2, 0)
        quantise_q_along_tokens(0, half(0))
        quantise_q_along_width(0, 1)
        regroup_q(on_scalar, 0, piece(1, 3, 4))
        regroup_q(on_vector, 0, piece(1, 0, 2))
        regroup_q(on_vector, 0, piece(1, 2, 4))
        quantise_q_along_width(2, 1)
        for i in (0, 2):
            for h in range(WIDTH_PASSES):
                flip_two_mem_tiles(i, h, on_scalar)
        quantise_q_along_tokens(0, half(1))
        flip_two_tiles(4, 0, on_scalar)
        flip_two_tiles(4, 1, on_scalar)
        quantise_mem(0)
        quantise_mem(1)
        quantise_q_along_width(4, 0)
        regroup_q(on_vector, 1, piece(0, 0, 4))
        flip_two_tiles(6, 0, on_scalar)
        flip_two_tiles(6, 1, on_scalar)
        regroup_q(on_scalar, 1, piece(0, 2, 4))
        regroup_q(on_scalar, 1, piece(1, 0, 4))
        quantise_q_along_width(4, 1)
        multiply_scores(4)
        multiply_scores(5)
        regroup_q(on_vector, 1, piece(0, 1, 4))
        quantise_q_along_width(6, 0)
        regroup_q(on_vector, 1, piece(0, 3, 4))
        quantise_q_along_width(6, 1)
        nc.vector.memset(gate[:], 1.0)
        for x in range(1, 4):
            regroup_q(on_gpsimd, 1, piece(1, x, 4))
        for k in (0, 1, 2, 3, 6, 7):
            multiply_scores(k)
        maximum(4)
        exponential(4)
        maximum(5)
        exponential(5)
        maximum(0)
        exponential(0)
        maximum(1)
        reciprocals_of(4, 2)
        scale(4)
        scale(5)
        exponential(1)
        maximum(2)
        exponential(2)
        maximum(3)
        exponential(3)
        reciprocals_of(0, 2)
        maximum(6)
        exponential(6)
        maximum(7)
        exponential(7)
        scale_and_floor(nc.vector, 0)
        reciprocals_of(2, 2)
        scale_and_floor(nc.vector, 1)
        reciprocals_of(6, 1)
        scale_on_scalar(6)
        scale_and_floor(nc.vector, 2)
        scale_and_floor(nc.vector, 3)
        quantise_q_along_tokens(1, piece(0, 0, 2))
        reciprocals_of(7, 1)
        quantise_q_along_tokens(1, piece(0, 1, 2))
        regroup_p(on_scalar, 0, 0)
        regroup_p(on_scalar, 0, 1)
        regroup_p(on_scalar, 0, 2)
        scale_and_floor(nc.vector, 7)
        keep_clock([p_rows[:, k // PACK, k % PACK, :] for k in (0, 1, 2, 3, 6)])
        quantise_p(0, 0)
        regroup_p(floor_on_vector, 1, 0)
        quantise_p(0, 1)
        quantise_p(1, 0)
        quantise_q_along_tokens(1, piece(1, 0, 2))
        regroup_p(floor_on_vector, 1, 1)
        quantise_q_along_tokens(1, piece(1, 1, 2))
        quantise_p(1, 1)
        quantise_p(0, 2)
        regroup_p(floor_on_vector, 1, 2)
        regroup_p(on_vector, 0, 3)
        regroup_p(floor_on_vector, 1, 3)
        quantise_p(1, 2)
        quantise_p(0, 3)
        quantise_p(1, 3)
        for x in range(2):
            first_pass(0, piece(0, x, 2))
        for x in range(2):
            first_pass(0, piece(1, x, 2))
        for x in range(2):
            last_pass_and_store(0, piece(0, x, 2), on_scalar)
        last_pass_and_store(0, piece(1, 0, 2), on_scalar)
        first_pass(1, half(0))
        last_pass_and_store(0, piece(1, 1, 2), on_scalar)
        last_pass_and_store(1, half(0), on_scalar)
        first_pass(1, half(1))
        last_pass_and_store(1, half(1), on_scalar)
        for i in range(2, SLOT_TILES):
            for n in range(WIDTH_HALVES):
                first_pass(i, half(n))
                last_pass_and_store(i, half(n), [on_scalar, on_vector][n])
